import numpy as np
import ml_dtypes


def mxq(x, axis, fmt="e4m3"):
    dtype, down = {"e4m3": (ml_dtypes.float8_e4m3fn, 7), "e5m2": (ml_dtypes.float8_e5m2, 14)}[fmt]
    v = np.moveaxis(np.asarray(x, np.float32).astype(ml_dtypes.bfloat16).astype(np.float64), axis, -1)
    blocks = v.reshape(v.shape[:-1] + (-1, 32))
    amax = np.abs(blocks).max(-1, keepdims=True)
    byte = np.maximum(np.where(amax > 0, np.frexp(amax)[1] - 1 + 127, 0) - down, 1)
    scale = np.exp2(byte - 127.0)
    codes = (blocks / scale).astype(np.float32).astype(dtype).astype(np.float64)
    return np.moveaxis((codes * scale).reshape(v.shape), -1, axis)


WIDE = False


def mx_kscale(k):
    if not WIDE:
        return np.ones(k)
    levels = np.array([10, -10, 5, -5, 0])
    if k % 512:
        return np.exp2(np.random.permutation(np.resize(levels, k // 32))).repeat(32)
    a = np.empty((k // 512, 16))
    for p in range(k // 512):
        a[p, :8] = np.random.permutation(np.resize(levels, 8))
        for g in range(8):
            far = levels[np.abs(levels - a[p, g]) >= 10]
            a[p, g + 8] = far[np.random.randint(len(far))]
    return np.exp2(a.ravel()).repeat(32)


BF16 = ml_dtypes.bfloat16


def bf(x):
    return np.asarray(x, np.float32).astype(BF16)


def f64(x):
    return np.asarray(x).astype(np.float64)


B, L, E, H, HD, F, G = 4, 640, 1536, 12, 128, 3072, 3072


def sigmoid(v):
    return 1.0 / (1.0 + np.exp(-v))


def setup_inputs():
    s, t = mx_kscale(E), mx_kscale(F)
    return {"h_ffn": bf(np.random.standard_normal((B, L, E)) * s),
            "w1": bf(np.random.standard_normal((E, F)) / np.sqrt(E) / s[:, None] * t),
            "b1": bf(0.2 * np.random.standard_normal(F) * t),
            "wg": bf(np.random.standard_normal((F, G)) / np.sqrt(F) / t[:, None]),
            "bg": bf(0.2 * np.random.standard_normal(G)),
            "wl": bf(np.random.standard_normal((F, G)) / np.sqrt(F) / t[:, None]),
            "bl": bf(0.2 * np.random.standard_normal(G)),
            "beta": bf(1.5 + 0.1 * np.random.standard_normal(1))}


def reference(h_ffn, w1, b1, wg, bg, wl, bl, beta):
    u = (mxq(f64(h_ffn), 2, "e4m3") @ mxq(f64(w1), 0, "e4m3")) + f64(b1)
    uq = mxq(u, 2, "e4m3")
    gate = (uq @ mxq(f64(wg), 0, "e4m3")) + f64(bg)
    lin = (uq @ mxq(f64(wl), 0, "e4m3")) + f64(bl)
    return gate * sigmoid(f64(beta) * gate) * lin

@@ -1,0 +1,239 @@
+from contextlib import ExitStack
+
+import concourse.mybir as mybir
+from concourse.masks import make_identity
+
+F32 = mybir.dt.float32
+BF16 = mybir.dt.bfloat16
+U32 = mybir.dt.uint32
+U8 = mybir.dt.uint8
+FP8X4 = mybir.dt.float8_e4m3fn_x4
+ACT = mybir.ActivationFunctionType
+ALU = mybir.AluOpType
+
+P = 128
+PACK = 4
+KP = P * PACK
+NT = 512
+
+FLOPS = 2 * 2560 * 1536 * 3072 + 2 * 2 * 2560 * 3072 * 3072
+
+
+def tile_llamaselfattentionblock_pb_l_kernel(tc, h_ffn, w1, b1, wg, bg, wl, bl, beta, out):
+    nc = tc.nc
+    h2 = h_ffn.flatten_outer_dims()
+    o2 = out.flatten_outer_dims()
+    n_tok, e_dim = h2.shape
+    f_dim = w1.shape[1]
+    g_dim = wg.shape[1]
+    n_blk = n_tok // NT
+    n_mt = n_tok // P
+    e_pass = e_dim // KP
+    f_pass = f_dim // KP
+    g_chunks = g_dim // NT
+
+    with ExitStack() as ctx:
+        keep = ctx.enter_context(tc.tile_pool(name="keep", bufs=1))
+        raw_w_pool = ctx.enter_context(tc.tile_pool(name="raw_w", bufs=4))
+        grp_wv_pool = ctx.enter_context(tc.tile_pool(name="grp_wv", bufs=2))
+        grp_ws_pool = ctx.enter_context(tc.tile_pool(name="grp_ws", bufs=2))
+        wca_pool = ctx.enter_context(tc.tile_pool(name="wca", bufs=2 * f_pass))
+        wpa_pool = ctx.enter_context(tc.tile_pool(name="wpa", bufs=2))
+        psum = ctx.enter_context(tc.psum_pool(name="psum", bufs=8))
+
+        warm = keep.tile([P, 1], F32, name="warm")
+        nc.vector.memset(warm[:], 0.0)
+        nc.scalar.activation(out=warm[:], in_=warm[:], func=ACT.Sigmoid)
+        ident = keep.tile([P, P], F32, name="ident")
+        make_identity(nc, ident[:])
+        b1_raw = keep.tile([P, f_pass, PACK], BF16, name="b1_raw")
+        nc.scalar.dma_start(out=b1_raw[:], in_=b1.rearrange("(c p t) -> p c t", p=P, t=PACK))
+        b1_col = keep.tile([P, f_pass * PACK], F32, name="b1_col")
+        nc.vector.tensor_copy(out=b1_col[:], in_=b1_raw[:].rearrange("p c t -> p (c t)"))
+        beta_raw = keep.tile([P, 1], BF16, name="beta_raw")
+        nc.scalar.dma_start(out=beta_raw[:], in_=beta.partition_broadcast(P))
+        beta_col = keep.tile([P, 1], F32, name="beta_col")
+        nc.vector.tensor_copy(out=beta_col[:], in_=beta_raw[:])
+        bg_all = keep.tile([P, g_dim], BF16, name="bg_all")
+        bl_all = keep.tile([P, g_dim], BF16, name="bl_all")
+
+        u_codes = []
+        for c in range(f_pass):
+            uc = keep.tile([P, n_tok], U32, name="uc%d" % c, align_bytes=64)
+            u_codes.append(uc)
+        u_planes = []
+        for c in range((f_pass + 3) // 4):
+            up = keep.tile([P, n_tok], U8, name="up%d" % c, align_bytes=64)
+            u_planes.append(up)
+
+        def quantize(grp, codes, plane):
+            nc.vector.quantize_mx(out=codes.bitcast(FP8X4), scales=plane, in_=grp)
+
+        def copy_on(vector, dst, src):
+            if vector:
+                nc.vector.tensor_copy(out=dst, in_=src)
+            else:
+                nc.scalar.copy(out=dst, in_=src)
+
+        def prep_weight(w, k_pass, col0, permute, vector, codes, plane):
+            raw = raw_w_pool.tile([P, PACK, NT], BF16, name="raw_w")
+            nc.sync.dma_start(
+                out=raw[:],
+                in_=w[k_pass * KP : (k_pass + 1) * KP, col0 : col0 + NT].rearrange("(p j) n -> p j n", j=PACK),
+            )
+            grp_pool = grp_wv_pool if vector else grp_ws_pool
+            grp = grp_pool.tile([P, NT * PACK], BF16, name="grp_w", align_bytes=64)
+            if permute:
+                dst = grp[:].rearrange("p (t m j) -> p t m j", t=PACK, j=PACK)
+                src = raw[:].rearrange("p j (m t) -> p t m j", t=PACK)
+            else:
+                dst = grp[:].rearrange("p (n j) -> p n j", j=PACK)
+                src = raw[:].rearrange("p j n -> p n j")
+            copy_on(vector, dst, src)
+            quantize(grp[:], codes, plane)
+
+        def prep_chunk(q, code_pool, plane_pool, vector_of):
+            chunk = []
+            for w, tag in ((wg, "g"), (wl, "l")):
+                planes = plane_pool.tile([P, 2, NT], U8, name="wp", align_bytes=64)
+                units = []
+                for c in range(f_pass):
+                    codes = code_pool.tile([P, NT], U32, name="wc", align_bytes=64)
+                    plane = planes[4 * (c % 4) :, c // 4, :]
+                    prep_weight(w, c, q * NT, False, vector_of(c), codes[:], plane)
+                    units.append((codes, plane))
+                chunk.append(units)
+            return chunk
+
+        with ExitStack() as s1:
+            w1c_pool = s1.enter_context(tc.tile_pool(name="w1c", bufs=3 * e_pass))
+            w1p_pool = s1.enter_context(tc.tile_pool(name="w1p", bufs=3))
+            h_keep = s1.enter_context(tc.tile_pool(name="h_keep", bufs=1))
+            raw_h_pool = s1.enter_context(tc.tile_pool(name="raw_h", bufs=6))
+            grp_av_pool = s1.enter_context(tc.tile_pool(name="grp_av", bufs=2))
+            grp_as_pool = s1.enter_context(tc.tile_pool(name="grp_as", bufs=2))
+            ust_pool = s1.enter_context(tc.tile_pool(name="ust", bufs=2))
+
+            h_codes = {}
+            h_planes = {}
+
+            def prep_h(n):
+                hp = h_keep.tile([P, NT], U8, name="hp%d" % n, align_bytes=64)
+                h_planes[n] = hp
+                for g in range(e_pass):
+                    hc = h_keep.tile([P, NT], U32, name="hc%d_%d" % (n, g), align_bytes=64)
+                    h_codes[(n, g)] = hc
+                for b in range(2):
+                    raws = []
+                    for a in range(2):
+                        m = 4 * n + 2 * b + a
+                        hr = raw_h_pool.tile([P, e_dim], BF16, name="raw_h")
+                        nc.sync.dma_start(out=hr[:], in_=h2[m * P : (m + 1) * P, :])
+                        raws.append(hr)
+                    for g in range(e_pass):
+                        xt = psum.tile([P, 2, 2, P], F32, name="ps")
+                        for a in range(2):
+                            words = raws[a][:].bitcast(F32)
+                            for u in range(2):
+                                nc.tensor.transpose(
+                                    xt[:, a, u, :], words[:, 256 * g + u : 256 * (g + 1) : 2], ident[:]
+                                )
+                        vector = (b + g) % 2 == 0
+                        grp_pool = grp_av_pool if vector else grp_as_pool
+                        grp = grp_pool.tile([P, NT * 2], BF16, name="grp_a", align_bytes=64)
+                        half = grp[:]
+                        copy_on(
+                            vector,
+                            half.bitcast(F32).rearrange("p (a r u) -> p a r u", a=2, u=2),
+                            xt[:].rearrange("p a u r -> p a r u"),
+                        )
+                        cols = slice(256 * b, 256 * (b + 1))
+                        quantize(half, h_codes[(n, g)][:, cols], hp[4 * g :, cols])
+
+            def tile1(n, c, w_units):
+                ust = ust_pool.tile([P, PACK, NT], BF16, name="ust")
+                for t in range(PACK):
+                    ps = psum.tile([P, NT], F32, name="ps")
+                    cols = slice(P * t, P * (t + 1))
+                    for g in range(e_pass):
+                        codes, plane = w_units[g]
+                        nc.tensor.matmul_mx(
+                            out=ps[:],
+                            lhsT=codes[:, cols].bitcast(FP8X4),
+                            lhsT_scale=plane[:, cols],
+                            rhs=h_codes[(n, g)][:].bitcast(FP8X4),
+                            rhs_scale=h_planes[n][4 * g :, :],
+                            start=(g == 0),
+                            stop=(g == e_pass - 1),
+                        )
+                    col = PACK * c + t
+                    nc.scalar.activation(
+                        out=ust[:, t, :], in_=ps[:], func=ACT.Identity, bias=b1_col[:, col : col + 1]
+                    )
+                grp = grp_av_pool.tile([P, NT * PACK], BF16, name="grp_a", align_bytes=64)
+                nc.vector.tensor_copy(
+                    out=grp[:].rearrange("p (n t) -> p n t", t=PACK), in_=ust[:].rearrange("p t n -> p n t")
+                )
+                cols = slice(NT * n, NT * (n + 1))
+                quantize(grp[:], u_codes[c][:, cols], u_planes[c // 4][4 * (c % 4) :, cols])
+
+            for c in range(f_pass):
+                planes = w1p_pool.tile([P, NT], U8, name="w1p", align_bytes=64)
+                w_units = []
+                if c == 0:
+                    prep_h(0)
+                for g in range(e_pass):
+                    codes = w1c_pool.tile([P, NT], U32, name="w1c", align_bytes=64)
+                    plane = planes[4 * g :, :]
+                    prep_weight(w1, g, c * NT, True, g != 2, codes[:], plane)
+                    w_units.append((codes, plane))
+                for n in range(n_blk):
+                    if c == 0 and n > 0:
+                        prep_h(n)
+                    tile1(n, c, w_units)
+
+            nc.sync.dma_start(out=bg_all[:], in_=bg.partition_broadcast(P))
+            nc.sync.dma_start(out=bl_all[:], in_=bl.partition_broadcast(P))
+            chunks = {0: prep_chunk(0, wca_pool, wpa_pool, lambda c: c % 3 != 2)}
+
+        with ExitStack() as s2:
+            wcb_pool = s2.enter_context(tc.tile_pool(name="wcb", bufs=4 * f_pass))
+            wpb_pool = s2.enter_context(tc.tile_pool(name="wpb", bufs=4))
+            g_pool = s2.enter_context(tc.tile_pool(name="g_sb", bufs=2))
+            l_pool = s2.enter_context(tc.tile_pool(name="l_sb", bufs=3))
+            s_pool = s2.enter_context(tc.tile_pool(name="s_sb", bufs=4))
+
+            for q in range(g_chunks):
+                units_g, units_l = chunks[q]
+                gcols = slice(q * NT, (q + 1) * NT)
+                for m in range(n_mt):
+                    tcols = slice(m * P, (m + 1) * P)
+                    banks = []
+                    for units in (units_g, units_l):
+                        ps = psum.tile([P, NT], F32, name="ps")
+                        for c in range(f_pass):
+                            codes, plane = units[c]
+                            nc.tensor.matmul_mx(
+                                out=ps[:],
+                                lhsT=u_codes[c][:, tcols].bitcast(FP8X4),
+                                lhsT_scale=u_planes[c // 4][4 * (c % 4) :, tcols],
+                                rhs=codes[:].bitcast(FP8X4),
+                                rhs_scale=plane,
+                                start=(c == 0),
+                                stop=(c == f_pass - 1),
+                            )
+                        banks.append(ps)
+                    g_sb = g_pool.tile([P, NT], F32, name="g_sb")
+                    nc.vector.tensor_tensor(out=g_sb[:], in0=banks[0][:], in1=bg_all[:, gcols], op=ALU.add)
+                    s_sb = s_pool.tile([P, NT], F32, name="s_sb")
+                    nc.scalar.activation(out=s_sb[:], in_=g_sb[:], func=ACT.Sigmoid, scale=beta_col[:, 0:1])
+                    l_sb = l_pool.tile([P, NT], F32, name="l_sb")
+                    nc.vector.tensor_tensor(out=l_sb[:], in0=banks[1][:], in1=bl_all[:, gcols], op=ALU.add)
+                    nc.vector.tensor_tensor(out=l_sb[:], in0=g_sb[:], in1=l_sb[:], op=ALU.mult)
+                    nc.vector.tensor_tensor(out=s_sb[:], in0=l_sb[:], in1=s_sb[:], op=ALU.mult)
+                    nc.gpsimd.dma_start(out=o2[tcols, gcols], in_=s_sb[:])
+                if q + 1 < g_chunks:
+                    if (q + 1) % 3 == 0:
+                        chunks[q + 1] = prep_chunk(q + 1, wca_pool, wpa_pool, lambda c: False)
+                    else:
+                        chunks[q + 1] = prep_chunk(q + 1, wcb_pool, wpb_pool, lambda c: False)

@@ -16,6 +16,19 @@ PACK = 4
 KP = P * PACK
 NT = 512
 
+RAW_W_BUFS = 4
+UST_BUFS = 2
+LOAD_AHEAD = 1
+S_PARTS_ROW0 = 2
+S_PARTS = 1
+BIAS_LOAD_STEP = 12
+
+
+def v_units(i, n_blk):
+    if i < n_blk:
+        return 1
+    return 1 if i % 3 else 0
+
 FLOPS = 2 * 2560 * 1536 * 3072 + 2 * 2 * 2560 * 3072 * 3072
 
 
@@ -32,9 +45,12 @@ def tile_llamaselfattentionblock_pb_l_kernel(tc, h_ffn, w1, b1, wg, bg, wl, bl, 
     f_pass = f_dim // KP
     g_chunks = g_dim // NT
 
+    n_steps1 = f_pass * n_blk
+    n_steps2 = g_chunks * n_mt
+
     with ExitStack() as ctx:
         keep = ctx.enter_context(tc.tile_pool(name="keep", bufs=1))
-        raw_w_pool = ctx.enter_context(tc.tile_pool(name="raw_w", bufs=4))
+        raw_w_pool = ctx.enter_context(tc.tile_pool(name="raw_w", bufs=RAW_W_BUFS))
         grp_wv_pool = ctx.enter_context(tc.tile_pool(name="grp_wv", bufs=2))
         grp_ws_pool = ctx.enter_context(tc.tile_pool(name="grp_ws", bufs=2))
         wca_pool = ctx.enter_context(tc.tile_pool(name="wca", bufs=2 * f_pass))
@@ -48,12 +64,10 @@ def tile_llamaselfattentionblock_pb_l_kernel(tc, h_ffn, w1, b1, wg, bg, wl, bl, 
         make_identity(nc, ident[:])
         b1_raw = keep.tile([P, f_pass, PACK], BF16, name="b1_raw")
         nc.scalar.dma_start(out=b1_raw[:], in_=b1.rearrange("(c p t) -> p c t", p=P, t=PACK))
-        b1_col = keep.tile([P, f_pass * PACK], F32, name="b1_col")
-        nc.vector.tensor_copy(out=b1_col[:], in_=b1_raw[:].rearrange("p c t -> p (c t)"))
         beta_raw = keep.tile([P, 1], BF16, name="beta_raw")
         nc.scalar.dma_start(out=beta_raw[:], in_=beta.partition_broadcast(P))
+        b1_col = keep.tile([P, f_pass * PACK], F32, name="b1_col")
         beta_col = keep.tile([P, 1], F32, name="beta_col")
-        nc.vector.tensor_copy(out=beta_col[:], in_=beta_raw[:])
         bg_all = keep.tile([P, g_dim], BF16, name="bg_all")
         bl_all = keep.tile([P, g_dim], BF16, name="bl_all")
 
@@ -66,174 +80,380 @@ def tile_llamaselfattentionblock_pb_l_kernel(tc, h_ffn, w1, b1, wg, bg, wl, bl, 
             up = keep.tile([P, n_tok], U8, name="up%d" % c, align_bytes=64)
             u_planes.append(up)
 
+        ctx.enter_context(tc.manual_schedule())
+
         def quantize(grp, codes, plane):
             nc.vector.quantize_mx(out=codes.bitcast(FP8X4), scales=plane, in_=grp)
 
-        def copy_on(vector, dst, src):
-            if vector:
-                nc.vector.tensor_copy(out=dst, in_=src)
-            else:
-                nc.scalar.copy(out=dst, in_=src)
-
-        def prep_weight(w, k_pass, col0, permute, vector, codes, plane):
+        def job_load(job):
             raw = raw_w_pool.tile([P, PACK, NT], BF16, name="raw_w")
+            k0 = job["k_pass"] * KP
             nc.sync.dma_start(
                 out=raw[:],
-                in_=w[k_pass * KP : (k_pass + 1) * KP, col0 : col0 + NT].rearrange("(p j) n -> p j n", j=PACK),
+                in_=job["w"][k0 : k0 + KP, job["col0"] : job["col0"] + NT].rearrange("(p j) n -> p j n", j=PACK),
             )
-            grp_pool = grp_wv_pool if vector else grp_ws_pool
-            grp = grp_pool.tile([P, NT * PACK], BF16, name="grp_w", align_bytes=64)
-            if permute:
-                dst = grp[:].rearrange("p (t m j) -> p t m j", t=PACK, j=PACK)
-                src = raw[:].rearrange("p j (m t) -> p t m j", t=PACK)
-            else:
-                dst = grp[:].rearrange("p (n j) -> p n j", j=PACK)
-                src = raw[:].rearrange("p j n -> p n j")
-            copy_on(vector, dst, src)
-            quantize(grp[:], codes, plane)
+            job["raw"] = raw
 
-        def prep_chunk(q, code_pool, plane_pool, vector_of):
-            chunk = []
-            for w, tag in ((wg, "g"), (wl, "l")):
-                planes = plane_pool.tile([P, 2, NT], U8, name="wp", align_bytes=64)
-                units = []
-                for c in range(f_pass):
+        def job_views(job, grp):
+            if job["permute"]:
+                dst = grp[:].rearrange("p (t m j) -> p t m j", t=PACK, j=PACK)
+                src = job["raw"][:].rearrange("p j (m t) -> p t m j", t=PACK)
+            else:
+                dst = grp[:].rearrange("p (t m j) -> p t m j", t=PACK, j=PACK)
+                src = job["raw"][:].rearrange("p j (t m) -> p t m j", t=PACK)
+            return dst, src
+
+        def job_copy_vector(job):
+            grp = grp_wv_pool.tile([P, NT * PACK], BF16, name="grp_w", align_bytes=64)
+            job["grp"] = grp
+            dst, src = job_views(job, grp)
+            nc.vector.tensor_copy(out=dst, in_=src)
+
+        def job_copy_scalar(job, part, parts):
+            if part == 0:
+                grp = grp_ws_pool.tile([P, NT * PACK], BF16, name="grp_w", align_bytes=64)
+                job["grp"] = grp
+            dst, src = job_views(job, job["grp"])
+            span = PACK // parts
+            sel = slice(part * span, (part + 1) * span)
+            nc.scalar.copy(out=dst[:, sel], in_=src[:, sel])
+
+        def job_quant(job):
+            codes, plane = job["target"]()
+            quantize(job["grp"][:], codes[:], plane)
+
+        chunks = {}
+
+        def chunk_jobs(q, code_pool, plane_pool):
+            chunks[q] = ({}, {})
+            jobs = []
+            for which, w in enumerate((wg, wl)):
+                holder = {}
+
+                def target(c, which=which, holder=holder):
+                    if "planes" not in holder:
+                        planes = plane_pool.tile([P, 2, NT], U8, name="wp", align_bytes=64)
+                        holder["planes"] = planes
                     codes = code_pool.tile([P, NT], U32, name="wc", align_bytes=64)
-                    plane = planes[4 * (c % 4) :, c // 4, :]
-                    prep_weight(w, c, q * NT, False, vector_of(c), codes[:], plane)
-                    units.append((codes, plane))
-                chunk.append(units)
-            return chunk
+                    plane = holder["planes"][4 * (c % 4) :, c // 4, :]
+                    chunks[q][which][c] = (codes, plane)
+                    return codes, plane
+
+                for c in range(f_pass):
+                    jobs.append(
+                        {"w": w, "k_pass": c, "col0": q * NT, "permute": False, "target": lambda c=c, f=target: f(c)}
+                    )
+            return jobs
 
         with ExitStack() as s1:
             w1c_pool = s1.enter_context(tc.tile_pool(name="w1c", bufs=3 * e_pass))
-            w1p_pool = s1.enter_context(tc.tile_pool(name="w1p", bufs=3))
+            w1p_pool = s1.enter_context(tc.tile_pool(name="w1p", bufs=e_pass + 2))
             h_keep = s1.enter_context(tc.tile_pool(name="h_keep", bufs=1))
             raw_h_pool = s1.enter_context(tc.tile_pool(name="raw_h", bufs=6))
             grp_av_pool = s1.enter_context(tc.tile_pool(name="grp_av", bufs=2))
-            grp_as_pool = s1.enter_context(tc.tile_pool(name="grp_as", bufs=2))
-            ust_pool = s1.enter_context(tc.tile_pool(name="ust", bufs=2))
+            grp_as_pool = s1.enter_context(tc.tile_pool(name="grp_as", bufs=3))
+            ust_pool = s1.enter_context(tc.tile_pool(name="ust", bufs=UST_BUFS))
 
             h_codes = {}
             h_planes = {}
-
-            def prep_h(n):
+            for n in range(n_blk):
                 hp = h_keep.tile([P, NT], U8, name="hp%d" % n, align_bytes=64)
                 h_planes[n] = hp
                 for g in range(e_pass):
                     hc = h_keep.tile([P, NT], U32, name="hc%d_%d" % (n, g), align_bytes=64)
                     h_codes[(n, g)] = hc
-                for b in range(2):
-                    raws = []
-                    for a in range(2):
-                        m = 4 * n + 2 * b + a
-                        hr = raw_h_pool.tile([P, e_dim], BF16, name="raw_h")
-                        nc.sync.dma_start(out=hr[:], in_=h2[m * P : (m + 1) * P, :])
-                        raws.append(hr)
-                    for g in range(e_pass):
-                        xt = psum.tile([P, 2, 2, P], F32, name="ps")
-                        for a in range(2):
-                            words = raws[a][:].bitcast(F32)
-                            for u in range(2):
-                                nc.tensor.transpose(
-                                    xt[:, a, u, :], words[:, 256 * g + u : 256 * (g + 1) : 2], ident[:]
-                                )
-                        vector = (b + g) % 2 == 0
-                        grp_pool = grp_av_pool if vector else grp_as_pool
-                        grp = grp_pool.tile([P, NT * 2], BF16, name="grp_a", align_bytes=64)
-                        half = grp[:]
-                        copy_on(
-                            vector,
-                            half.bitcast(F32).rearrange("p (a r u) -> p a r u", a=2, u=2),
-                            xt[:].rearrange("p a u r -> p a r u"),
-                        )
-                        cols = slice(256 * b, 256 * (b + 1))
-                        quantize(half, h_codes[(n, g)][:, cols], hp[4 * g :, cols])
 
-            def tile1(n, c, w_units):
+            w1_units = {}
+            w1_planes = {}
+
+            def w1_job(c, g):
+                def target():
+                    codes = w1c_pool.tile([P, NT], U32, name="w1c", align_bytes=64)
+                    if c == 0:
+                        planes = w1p_pool.tile([P, NT], U8, name="w1p", align_bytes=64)
+                        plane = planes[:]
+                    else:
+                        if c not in w1_planes:
+                            planes = w1p_pool.tile([P, NT], U8, name="w1p", align_bytes=64)
+                            w1_planes[c] = planes
+                        plane = w1_planes[c][4 * g :, :]
+                    w1_units[(c, g)] = (codes, plane)
+                    return codes, plane
+
+                return {"w": w1, "k_pass": g, "col0": c * NT, "permute": True, "target": target, "chunk": c}
+
+            h_raws = {}
+
+            def h_load(hb):
+                if hb >= 2 * n_blk:
+                    return
+                raws = []
+                for a in range(2):
+                    m = 2 * hb + a
+                    hr = raw_h_pool.tile([P, e_dim], BF16, name="raw_h")
+                    nc.sync.dma_start(out=hr[:], in_=h2[m * P : (m + 1) * P, :])
+                    raws.append(hr)
+                h_raws[hb] = raws
+
+            def h_transpose(hb, share):
+                todo = []
+                n, b = hb // 2, hb % 2
+                for g in range(e_pass):
+                    xt = psum.tile([P, 2, 2, P], F32, name="ps")
+                    for a in range(2):
+                        words = h_raws[hb][a][:].bitcast(F32)
+                        for u in range(2):
+                            nc.tensor.transpose(xt[:, a, u, :], words[:, 256 * g + u : 256 * (g + 1) : 2], ident[:])
+                    on_vector = share and g % 2 == 1
+                    grp_pool = grp_av_pool if on_vector else grp_as_pool
+                    grp = grp_pool.tile([P, NT * 2], BF16, name="grp_a", align_bytes=64)
+                    dst = grp[:].bitcast(F32).rearrange("p (a r u) -> p a r u", a=2, u=2)
+                    src = xt[:].rearrange("p a u r -> p a r u")
+                    if on_vector:
+                        nc.vector.tensor_copy(out=dst, in_=src)
+                    else:
+                        nc.scalar.copy(out=dst, in_=src)
+                    cols = slice(256 * b, 256 * (b + 1))
+                    todo.append((grp[:], h_codes[(n, g)][:, cols], h_planes[n][4 * g :, cols]))
+                h_load(hb + 3)
+                return todo
+
+            usts = {}
+
+            def pass1(i, t, g, ps):
+                c, n = i // n_blk, i % n_blk
+                cols = slice(P * t, P * (t + 1))
+                codes, plane = w1_units[(c, g)]
+                nc.tensor.matmul_mx(
+                    out=ps[:],
+                    lhsT=codes[:, cols].bitcast(FP8X4),
+                    lhsT_scale=plane[:, cols],
+                    rhs=h_codes[(n, g)][:].bitcast(FP8X4),
+                    rhs_scale=h_planes[n][4 * g :, :],
+                    start=(g == 0),
+                    stop=(g == e_pass - 1),
+                )
+
+            def evacuate1(i, t, ps):
+                col = PACK * (i // n_blk) + t
+                nc.scalar.activation(
+                    out=usts[i][:, t, :], in_=ps[:], func=ACT.Identity, bias=b1_col[:, col : col + 1]
+                )
+
+            def tile1(i):
                 ust = ust_pool.tile([P, PACK, NT], BF16, name="ust")
+                usts[i] = ust
                 for t in range(PACK):
                     ps = psum.tile([P, NT], F32, name="ps")
-                    cols = slice(P * t, P * (t + 1))
                     for g in range(e_pass):
-                        codes, plane = w_units[g]
-                        nc.tensor.matmul_mx(
-                            out=ps[:],
-                            lhsT=codes[:, cols].bitcast(FP8X4),
-                            lhsT_scale=plane[:, cols],
-                            rhs=h_codes[(n, g)][:].bitcast(FP8X4),
-                            rhs_scale=h_planes[n][4 * g :, :],
-                            start=(g == 0),
-                            stop=(g == e_pass - 1),
-                        )
-                    col = PACK * c + t
-                    nc.scalar.activation(
-                        out=ust[:, t, :], in_=ps[:], func=ACT.Identity, bias=b1_col[:, col : col + 1]
-                    )
+                        pass1(i, t, g, ps)
+                    evacuate1(i, t, ps)
+
+            u_grps = {}
+
+            def u_interleave(i):
                 grp = grp_av_pool.tile([P, NT * PACK], BF16, name="grp_a", align_bytes=64)
+                u_grps[i] = grp
                 nc.vector.tensor_copy(
-                    out=grp[:].rearrange("p (n t) -> p n t", t=PACK), in_=ust[:].rearrange("p t n -> p n t")
+                    out=grp[:].rearrange("p (n t) -> p n t", t=PACK), in_=usts[i][:].rearrange("p t n -> p n t")
                 )
+
+            def u_quant(i):
+                c, n = i // n_blk, i % n_blk
                 cols = slice(NT * n, NT * (n + 1))
-                quantize(grp[:], u_codes[c][:, cols], u_planes[c // 4][4 * (c % 4) :, cols])
+                quantize(u_grps[i][:], u_codes[c][:, cols], u_planes[c // 4][4 * (c % 4) :, cols])
 
-            for c in range(f_pass):
-                planes = w1p_pool.tile([P, NT], U8, name="w1p", align_bytes=64)
-                w_units = []
-                if c == 0:
-                    prep_h(0)
-                for g in range(e_pass):
-                    codes = w1c_pool.tile([P, NT], U32, name="w1c", align_bytes=64)
-                    plane = planes[4 * g :, :]
-                    prep_weight(w1, g, c * NT, True, g != 2, codes[:], plane)
-                    w_units.append((codes, plane))
-                for n in range(n_blk):
-                    if c == 0 and n > 0:
-                        prep_h(n)
-                    tile1(n, c, w_units)
+            w1_todo = [w1_job(c, g) for c in range(1, f_pass) for g in range(e_pass)]
+            s2_todo = chunk_jobs(0, wca_pool, wpa_pool)
 
-            nc.sync.dma_start(out=bg_all[:], in_=bg.partition_broadcast(P))
-            nc.sync.dma_start(out=bl_all[:], in_=bl.partition_broadcast(P))
-            chunks = {0: prep_chunk(0, wca_pool, wpa_pool, lambda c: c % 3 != 2)}
+            taken = {"w1": 0, "s2": 0}
+
+            def pop_job(i):
+                a, b = taken["w1"], taken["s2"]
+                if a < len(w1_todo) and i + 1 >= n_blk * (w1_todo[a]["chunk"] - 2):
+                    taken["w1"] = a + 1
+                    return w1_todo[a]
+                if b < len(s2_todo):
+                    taken["s2"] = b + 1
+                    return s2_todo[b]
+                return None
+
+            loads = {}
+            v_copy = {}
+            s_copy = {}
+            quants = {}
+            s_job = None
+            s_done = 0
+            n_plan = n_steps1
+            i = -1
+            while i + 1 < n_plan:
+                i += 1
+                if i == n_plan - 1 and (taken["w1"] < len(w1_todo) or taken["s2"] < len(s2_todo) or s_job is not None):
+                    n_plan += 1
+                for k in range(S_PARTS_ROW0 if i < n_blk else S_PARTS):
+                    if s_job is None:
+                        s_job = pop_job(i)
+                        s_done = 0
+                        if s_job is not None:
+                            loads[i - LOAD_AHEAD] = loads.get(i - LOAD_AHEAD, []) + [s_job]
+                    if s_job is not None:
+                        s_copy[i] = s_copy.get(i, []) + [(s_job, s_done)]
+                        s_done += 1
+                        if s_done == PACK:
+                            quants[i + 1] = quants.get(i + 1, []) + [s_job]
+                            s_job = None
+                for k in range(v_units(i, n_blk)):
+                    job = pop_job(i)
+                    if job is not None:
+                        loads[i - LOAD_AHEAD] = loads.get(i - LOAD_AHEAD, []) + [job]
+                        v_copy[i] = v_copy.get(i, []) + [job]
+                        quants[i + 1] = quants.get(i + 1, []) + [job]
+            assert taken["w1"] == len(w1_todo) and taken["s2"] == len(s2_todo) and s_job is None
+
+            first = [w1_job(0, g) for g in range(e_pass)]
+            h_load(0)
+            h_load(1)
+            for job in first:
+                job_load(job)
+            h_load(2)
+            nc.vector.tensor_copy(out=b1_col[:], in_=b1_raw[:].rearrange("p c t -> p (c t)"))
+            nc.vector.tensor_copy(out=beta_col[:], in_=beta_raw[:])
+            for hb in range(2):
+                for args in h_transpose(hb, False):
+                    quantize(*args)
+            ust = ust_pool.tile([P, PACK, NT], BF16, name="ust")
+            usts[0] = ust
+            banks0 = []
+            for t in range(PACK):
+                ps = psum.tile([P, NT], F32, name="ps")
+                banks0.append(ps)
+            for g in range(e_pass):
+                if g % 2 == 1:
+                    job_copy_scalar(first[g], 0, 1)
+                else:
+                    job_copy_vector(first[g])
+            for g in range(e_pass):
+                job_quant(first[g])
+                for t in range(PACK):
+                    pass1(0, t, g, banks0[t])
+            for t in range(PACK):
+                evacuate1(0, t, banks0[t])
+            for i in range(-LOAD_AHEAD, 0):
+                for job in loads.get(i, []):
+                    job_load(job)
+
+            for i in range(n_plan + 1):
+                for job in loads.get(i, []):
+                    job_load(job)
+                if i == min(BIAS_LOAD_STEP, n_steps1 - 1):
+                    nc.sync.dma_start(out=bg_all[:], in_=bg.partition_broadcast(P))
+                    nc.sync.dma_start(out=bl_all[:], in_=bl.partition_broadcast(P))
+                if 0 < i < n_steps1:
+                    tile1(i)
+                if 0 < i <= n_steps1:
+                    u_interleave(i - 1)
+                for job in quants.get(i, []):
+                    job_quant(job)
+                if 0 < i <= n_steps1:
+                    u_quant(i - 1)
+                for job in v_copy.get(i, []):
+                    job_copy_vector(job)
+                if i < n_blk:
+                    for hb in range(3 * i + 2, min(3 * i + 5, 2 * n_blk)):
+                        for args in h_transpose(hb, False):
+                            quantize(*args)
+                for job, part in s_copy.get(i, []):
+                    job_copy_scalar(job, part, PACK)
 
         with ExitStack() as s2:
-            wcb_pool = s2.enter_context(tc.tile_pool(name="wcb", bufs=4 * f_pass))
-            wpb_pool = s2.enter_context(tc.tile_pool(name="wpb", bufs=4))
+            wcb_pool = s2.enter_context(tc.tile_pool(name="wcb", bufs=2 * f_pass))
+            wpb_pool = s2.enter_context(tc.tile_pool(name="wpb", bufs=2))
             g_pool = s2.enter_context(tc.tile_pool(name="g_sb", bufs=2))
             l_pool = s2.enter_context(tc.tile_pool(name="l_sb", bufs=3))
             s_pool = s2.enter_context(tc.tile_pool(name="s_sb", bufs=4))
 
-            for q in range(g_chunks):
-                units_g, units_l = chunks[q]
-                gcols = slice(q * NT, (q + 1) * NT)
-                for m in range(n_mt):
-                    tcols = slice(m * P, (m + 1) * P)
-                    banks = []
-                    for units in (units_g, units_l):
-                        ps = psum.tile([P, NT], F32, name="ps")
-                        for c in range(f_pass):
-                            codes, plane = units[c]
-                            nc.tensor.matmul_mx(
-                                out=ps[:],
-                                lhsT=u_codes[c][:, tcols].bitcast(FP8X4),
-                                lhsT_scale=u_planes[c // 4][4 * (c % 4) :, tcols],
-                                rhs=codes[:].bitcast(FP8X4),
-                                rhs_scale=plane,
-                                start=(c == 0),
-                                stop=(c == f_pass - 1),
-                            )
-                        banks.append(ps)
-                    g_sb = g_pool.tile([P, NT], F32, name="g_sb")
-                    nc.vector.tensor_tensor(out=g_sb[:], in0=banks[0][:], in1=bg_all[:, gcols], op=ALU.add)
-                    s_sb = s_pool.tile([P, NT], F32, name="s_sb")
-                    nc.scalar.activation(out=s_sb[:], in_=g_sb[:], func=ACT.Sigmoid, scale=beta_col[:, 0:1])
-                    l_sb = l_pool.tile([P, NT], F32, name="l_sb")
-                    nc.vector.tensor_tensor(out=l_sb[:], in0=banks[1][:], in1=bl_all[:, gcols], op=ALU.add)
-                    nc.vector.tensor_tensor(out=l_sb[:], in0=g_sb[:], in1=l_sb[:], op=ALU.mult)
-                    nc.vector.tensor_tensor(out=s_sb[:], in0=l_sb[:], in1=s_sb[:], op=ALU.mult)
-                    nc.gpsimd.dma_start(out=o2[tcols, gcols], in_=s_sb[:])
-                if q + 1 < g_chunks:
-                    if (q + 1) % 3 == 0:
-                        chunks[q + 1] = prep_chunk(q + 1, wca_pool, wpa_pool, lambda c: False)
-                    else:
-                        chunks[q + 1] = prep_chunk(q + 1, wcb_pool, wpb_pool, lambda c: False)
+            loads = {}
+            copies = {}
+            quants = {}
+            for q in range(1, g_chunks):
+                if q % 2 == 0:
+                    jobs = chunk_jobs(q, wca_pool, wpa_pool)
+                else:
+                    jobs = chunk_jobs(q, wcb_pool, wpb_pool)
+                for j, job in enumerate(jobs):
+                    i = (q - 1) * n_mt + (j * (n_mt - 2)) // len(jobs)
+                    at = max(i - LOAD_AHEAD, 0)
+                    loads[at] = loads.get(at, []) + [job]
+                    copies[i] = copies.get(i, []) + [job]
+                    quants[i + 1] = quants.get(i + 1, []) + [job]
+
+            bank_g = {}
+            bank_l = {}
+            g_sb = {}
+            l_sb = {}
+            s_sb = {}
+
+            def matmuls(i, which, banks):
+                q, m = i // n_mt, i % n_mt
+                tcols = slice(m * P, (m + 1) * P)
+                ps = psum.tile([P, NT], F32, name="ps")
+                banks[i] = ps
+                for c in range(f_pass):
+                    codes, plane = chunks[q][which][c]
+                    nc.tensor.matmul_mx(
+                        out=ps[:],
+                        lhsT=u_codes[c][:, tcols].bitcast(FP8X4),
+                        lhsT_scale=u_planes[c // 4][4 * (c % 4) :, tcols],
+                        rhs=codes[:].bitcast(FP8X4),
+                        rhs_scale=plane,
+                        start=(c == 0),
+                        stop=(c == f_pass - 1),
+                    )
+
+            def gcols(i):
+                q = i // n_mt
+                return slice(q * NT, (q + 1) * NT)
+
+            def add_bg(i):
+                t = g_pool.tile([P, NT], F32, name="g_sb")
+                g_sb[i] = t
+                nc.vector.tensor_tensor(out=t[:], in0=bank_g[i][:], in1=bg_all[:, gcols(i)], op=ALU.add)
+
+            def sigmoid(i):
+                t = s_pool.tile([P, NT], F32, name="s_sb")
+                s_sb[i] = t
+                nc.scalar.activation(out=t[:], in_=g_sb[i][:], func=ACT.Sigmoid, scale=beta_col[:, 0:1])
+
+            def add_bl(i):
+                t = l_pool.tile([P, NT], F32, name="l_sb")
+                l_sb[i] = t
+                nc.vector.tensor_tensor(out=t[:], in0=bank_l[i][:], in1=bl_all[:, gcols(i)], op=ALU.add)
+
+            def gate_lin(i):
+                nc.vector.tensor_tensor(out=l_sb[i][:], in0=g_sb[i][:], in1=l_sb[i][:], op=ALU.mult)
+
+            def finish(i):
+                m = i % n_mt
+                nc.vector.tensor_tensor(out=s_sb[i][:], in0=l_sb[i][:], in1=s_sb[i][:], op=ALU.mult)
+                queue = nc.sync if i >= n_steps2 - n_mt else nc.gpsimd
+                queue.dma_start(out=o2[m * P : (m + 1) * P, gcols(i)], in_=s_sb[i][:])
+
+            for i in range(n_steps2 + 2):
+                for job in loads.get(i, []):
+                    job_load(job)
+                if i < n_steps2:
+                    matmuls(i, 0, bank_g)
+                    matmuls(i, 1, bank_l)
+                for job in copies.get(i, []):
+                    job_copy_scalar(job, 0, 1)
+                if 1 <= i <= n_steps2:
+                    add_bl(i - 1)
+                if i >= 2:
+                    finish(i - 2)
+                if 1 <= i <= n_steps2:
+                    gate_lin(i - 1)
+                if i < n_steps2:
+                    add_bg(i)
+                    sigmoid(i)
+                for job in quants.get(i, []):
+                    job_quant(job)

@@ -356,12 +356,12 @@ def tile_llamaselfattentionblock_pb_l_kernel(tc, h_ffn, w1, b1, wg, bg, wl, bl, 
                     job_quant(job)
                 if 0 < i <= n_steps1:
                     u_quant(i - 1)
-                for job in v_copy.get(i, []):
-                    job_copy_vector(job)
                 if i < n_blk:
                     for hb in range(3 * i + 2, min(3 * i + 5, 2 * n_blk)):
                         for args in h_transpose(hb, False):
                             quantize(*args)
+                for job in v_copy.get(i, []):
+                    job_copy_vector(job)
                 for job, part in s_copy.get(i, []):
                     job_copy_scalar(job, part, PACK)
 
@@ -432,13 +432,15 @@ def tile_llamaselfattentionblock_pb_l_kernel(tc, h_ffn, w1, b1, wg, bg, wl, bl, 
             def gate_lin(i):
                 nc.vector.tensor_tensor(out=l_sb[i][:], in0=g_sb[i][:], in1=l_sb[i][:], op=ALU.mult)
 
+            def gate_sigmoid(i):
+                nc.vector.tensor_tensor(out=s_sb[i][:], in0=g_sb[i][:], in1=s_sb[i][:], op=ALU.mult)
+
             def finish(i):
                 m = i % n_mt
                 nc.vector.tensor_tensor(out=s_sb[i][:], in0=l_sb[i][:], in1=s_sb[i][:], op=ALU.mult)
-                queue = nc.sync if i >= n_steps2 - n_mt else nc.gpsimd
-                queue.dma_start(out=o2[m * P : (m + 1) * P, gcols(i)], in_=s_sb[i][:])
+                nc.sync.dma_start(out=o2[m * P : (m + 1) * P, gcols(i)], in_=s_sb[i][:])
 
-            for i in range(n_steps2 + 2):
+            for i in range(n_steps2 + 1):
                 for job in loads.get(i, []):
                     job_load(job)
                 if i < n_steps2:
@@ -446,11 +448,17 @@ def tile_llamaselfattentionblock_pb_l_kernel(tc, h_ffn, w1, b1, wg, bg, wl, bl, 
                     matmuls(i, 1, bank_l)
                 for job in copies.get(i, []):
                     job_copy_scalar(job, 0, 1)
-                if 1 <= i <= n_steps2:
+                if i == n_steps2:
+                    finish(i - 2)
+                    gate_sigmoid(i - 1)
+                    add_bl(i - 1)
+                    finish(i - 1)
+                    break
+                if i >= 1:
                     add_bl(i - 1)
                 if i >= 2:
                     finish(i - 2)
-                if 1 <= i <= n_steps2:
+                if i >= 1:
                     gate_lin(i - 1)
                 if i < n_steps2:
                     add_bg(i)

@@ -371,6 +371,7 @@ def tile_llamaselfattentionblock_pb_l_kernel(tc, h_ffn, w1, b1, wg, bg, wl, bl, 
             g_pool = s2.enter_context(tc.tile_pool(name="g_sb", bufs=2))
             l_pool = s2.enter_context(tc.tile_pool(name="l_sb", bufs=3))
             s_pool = s2.enter_context(tc.tile_pool(name="s_sb", bufs=4))
+            last_pool = s2.enter_context(tc.tile_pool(name="l_last", bufs=1))
 
             loads = {}
             copies = {}
@@ -381,10 +382,12 @@ def tile_llamaselfattentionblock_pb_l_kernel(tc, h_ffn, w1, b1, wg, bg, wl, bl, 
                 else:
                     jobs = chunk_jobs(q, wcb_pool, wpb_pool)
                 for j, job in enumerate(jobs):
-                    i = (q - 1) * n_mt + (j * (n_mt - 2)) // len(jobs)
-                    at = max(i - LOAD_AHEAD, 0)
-                    loads[at] = loads.get(at, []) + [job]
-                    copies[i] = copies.get(i, []) + [job]
+                    for part in range(PACK):
+                        i = (q - 1) * n_mt + ((PACK * j + part) * (n_mt - 2)) // (PACK * len(jobs))
+                        if part == 0:
+                            at = max(i - LOAD_AHEAD, 0)
+                            loads[at] = loads.get(at, []) + [job]
+                        copies[i] = copies.get(i, []) + [(job, part)]
                     quants[i + 1] = quants.get(i + 1, []) + [job]
 
             bank_g = {}
@@ -424,8 +427,16 @@ def tile_llamaselfattentionblock_pb_l_kernel(tc, h_ffn, w1, b1, wg, bg, wl, bl, 
                 s_sb[i] = t
                 nc.scalar.activation(out=t[:], in_=g_sb[i][:], func=ACT.Sigmoid, scale=beta_col[:, 0:1])
 
-            def add_bl(i):
+            def copy_l(i):
                 t = l_pool.tile([P, NT], F32, name="l_sb")
+                l_sb[i] = t
+                nc.scalar.copy(out=t[:], in_=bank_l[i][:])
+
+            def add_bl(i):
+                nc.vector.tensor_tensor(out=l_sb[i][:], in0=l_sb[i][:], in1=bl_all[:, gcols(i)], op=ALU.add)
+
+            def add_bl_last(i):
+                t = last_pool.tile([P, NT], F32, name="l_last")
                 l_sb[i] = t
                 nc.vector.tensor_tensor(out=t[:], in0=bank_l[i][:], in1=bl_all[:, gcols(i)], op=ALU.add)
 
@@ -446,22 +457,23 @@ def tile_llamaselfattentionblock_pb_l_kernel(tc, h_ffn, w1, b1, wg, bg, wl, bl, 
                 if i < n_steps2:
                     matmuls(i, 0, bank_g)
                     matmuls(i, 1, bank_l)
-                for job in copies.get(i, []):
-                    job_copy_scalar(job, 0, 1)
                 if i == n_steps2:
                     finish(i - 2)
                     gate_sigmoid(i - 1)
-                    add_bl(i - 1)
+                    add_bl_last(i - 1)
                     finish(i - 1)
                     break
+                if i >= 1:
+                    copy_l(i - 1)
+                for job, part in copies.get(i, []):
+                    job_copy_scalar(job, part, PACK)
                 if i >= 1:
                     add_bl(i - 1)
                 if i >= 2:
                     finish(i - 2)
+                add_bg(i)
+                sigmoid(i)
                 if i >= 1:
                     gate_lin(i - 1)
-                if i < n_steps2:
-                    add_bg(i)
-                    sigmoid(i)
                 for job in quants.get(i, []):
                     job_quant(job)

@@ -73,11 +73,11 @@ def tile_llamaselfattentionblock_pb_l_kernel(tc, h_ffn, w1, b1, wg, bg, wl, bl, 
 
         u_codes = []
         for c in range(f_pass):
-            uc = keep.tile([P, n_tok], U32, name="uc%d" % c, align_bytes=64)
+            uc = keep.tile([P, n_tok], U32, name="uc%d" % c, align_bytes=256)
             u_codes.append(uc)
         u_planes = []
         for c in range((f_pass + 3) // 4):
-            up = keep.tile([P, n_tok], U8, name="up%d" % c, align_bytes=64)
+            up = keep.tile([P, n_tok], U8, name="up%d" % c, align_bytes=256)
             u_planes.append(up)
 
         ctx.enter_context(tc.manual_schedule())
@@ -104,14 +104,14 @@ def tile_llamaselfattentionblock_pb_l_kernel(tc, h_ffn, w1, b1, wg, bg, wl, bl, 
             return dst, src
 
         def job_copy_vector(job):
-            grp = grp_wv_pool.tile([P, NT * PACK], BF16, name="grp_w", align_bytes=64)
+            grp = grp_wv_pool.tile([P, NT * PACK], BF16, name="grp_w", align_bytes=256)
             job["grp"] = grp
             dst, src = job_views(job, grp)
             nc.vector.tensor_copy(out=dst, in_=src)
 
         def job_copy_scalar(job, part, parts):
             if part == 0:
-                grp = grp_ws_pool.tile([P, NT * PACK], BF16, name="grp_w", align_bytes=64)
+                grp = grp_ws_pool.tile([P, NT * PACK], BF16, name="grp_w", align_bytes=256)
                 job["grp"] = grp
             dst, src = job_views(job, job["grp"])
             span = PACK // parts
@@ -132,9 +132,9 @@ def tile_llamaselfattentionblock_pb_l_kernel(tc, h_ffn, w1, b1, wg, bg, wl, bl, 
 
                 def target(c, which=which, holder=holder):
                     if "planes" not in holder:
-                        planes = plane_pool.tile([P, 2, NT], U8, name="wp", align_bytes=64)
+                        planes = plane_pool.tile([P, 2, NT], U8, name="wp", align_bytes=256)
                         holder["planes"] = planes
-                    codes = code_pool.tile([P, NT], U32, name="wc", align_bytes=64)
+                    codes = code_pool.tile([P, NT], U32, name="wc", align_bytes=256)
                     plane = holder["planes"][4 * (c % 4) :, c // 4, :]
                     chunks[q][which][c] = (codes, plane)
                     return codes, plane
@@ -157,10 +157,10 @@ def tile_llamaselfattentionblock_pb_l_kernel(tc, h_ffn, w1, b1, wg, bg, wl, bl, 
             h_codes = {}
             h_planes = {}
             for n in range(n_blk):
-                hp = h_keep.tile([P, NT], U8, name="hp%d" % n, align_bytes=64)
+                hp = h_keep.tile([P, NT], U8, name="hp%d" % n, align_bytes=256)
                 h_planes[n] = hp
                 for g in range(e_pass):
-                    hc = h_keep.tile([P, NT], U32, name="hc%d_%d" % (n, g), align_bytes=64)
+                    hc = h_keep.tile([P, NT], U32, name="hc%d_%d" % (n, g), align_bytes=256)
                     h_codes[(n, g)] = hc
 
             w1_units = {}
@@ -168,13 +168,13 @@ def tile_llamaselfattentionblock_pb_l_kernel(tc, h_ffn, w1, b1, wg, bg, wl, bl, 
 
             def w1_job(c, g):
                 def target():
-                    codes = w1c_pool.tile([P, NT], U32, name="w1c", align_bytes=64)
+                    codes = w1c_pool.tile([P, NT], U32, name="w1c", align_bytes=256)
                     if c == 0:
-                        planes = w1p_pool.tile([P, NT], U8, name="w1p", align_bytes=64)
+                        planes = w1p_pool.tile([P, NT], U8, name="w1p", align_bytes=256)
                         plane = planes[:]
                     else:
                         if c not in w1_planes:
-                            planes = w1p_pool.tile([P, NT], U8, name="w1p", align_bytes=64)
+                            planes = w1p_pool.tile([P, NT], U8, name="w1p", align_bytes=256)
                             w1_planes[c] = planes
                         plane = w1_planes[c][4 * g :, :]
                     w1_units[(c, g)] = (codes, plane)
@@ -206,7 +206,7 @@ def tile_llamaselfattentionblock_pb_l_kernel(tc, h_ffn, w1, b1, wg, bg, wl, bl, 
                             nc.tensor.transpose(xt[:, a, u, :], words[:, 256 * g + u : 256 * (g + 1) : 2], ident[:])
                     on_vector = share and g % 2 == 1
                     grp_pool = grp_av_pool if on_vector else grp_as_pool
-                    grp = grp_pool.tile([P, NT * 2], BF16, name="grp_a", align_bytes=64)
+                    grp = grp_pool.tile([P, NT * 2], BF16, name="grp_a", align_bytes=256)
                     dst = grp[:].bitcast(F32).rearrange("p (a r u) -> p a r u", a=2, u=2)
                     src = xt[:].rearrange("p a u r -> p a r u")
                     if on_vector:
@@ -252,7 +252,7 @@ def tile_llamaselfattentionblock_pb_l_kernel(tc, h_ffn, w1, b1, wg, bg, wl, bl, 
             u_grps = {}
 
             def u_interleave(i):
-                grp = grp_av_pool.tile([P, NT * PACK], BF16, name="grp_a", align_bytes=64)
+                grp = grp_av_pool.tile([P, NT * PACK], BF16, name="grp_a", align_bytes=256)
                 u_grps[i] = grp
                 nc.vector.tensor_copy(
                     out=grp[:].rearrange("p (n t) -> p n t", t=PACK), in_=usts[i][:].rearrange("p t n -> p n t")
@@ -371,7 +371,6 @@ def tile_llamaselfattentionblock_pb_l_kernel(tc, h_ffn, w1, b1, wg, bg, wl, bl, 
             g_pool = s2.enter_context(tc.tile_pool(name="g_sb", bufs=2))
             l_pool = s2.enter_context(tc.tile_pool(name="l_sb", bufs=3))
             s_pool = s2.enter_context(tc.tile_pool(name="s_sb", bufs=4))
-            last_pool = s2.enter_context(tc.tile_pool(name="l_last", bufs=1))
 
             loads = {}
             copies = {}
@@ -382,12 +381,10 @@ def tile_llamaselfattentionblock_pb_l_kernel(tc, h_ffn, w1, b1, wg, bg, wl, bl, 
                 else:
                     jobs = chunk_jobs(q, wcb_pool, wpb_pool)
                 for j, job in enumerate(jobs):
-                    for part in range(PACK):
-                        i = (q - 1) * n_mt + ((PACK * j + part) * (n_mt - 2)) // (PACK * len(jobs))
-                        if part == 0:
-                            at = max(i - LOAD_AHEAD, 0)
-                            loads[at] = loads.get(at, []) + [job]
-                        copies[i] = copies.get(i, []) + [(job, part)]
+                    i = (q - 1) * n_mt + (j * (n_mt - 2)) // len(jobs)
+                    at = max(i - LOAD_AHEAD, 0)
+                    loads[at] = loads.get(at, []) + [job]
+                    copies[i] = copies.get(i, []) + [job]
                     quants[i + 1] = quants.get(i + 1, []) + [job]
 
             bank_g = {}
@@ -427,16 +424,8 @@ def tile_llamaselfattentionblock_pb_l_kernel(tc, h_ffn, w1, b1, wg, bg, wl, bl, 
                 s_sb[i] = t
                 nc.scalar.activation(out=t[:], in_=g_sb[i][:], func=ACT.Sigmoid, scale=beta_col[:, 0:1])
 
-            def copy_l(i):
-                t = l_pool.tile([P, NT], F32, name="l_sb")
-                l_sb[i] = t
-                nc.scalar.copy(out=t[:], in_=bank_l[i][:])
-
             def add_bl(i):
-                nc.vector.tensor_tensor(out=l_sb[i][:], in0=l_sb[i][:], in1=bl_all[:, gcols(i)], op=ALU.add)
-
-            def add_bl_last(i):
-                t = last_pool.tile([P, NT], F32, name="l_last")
+                t = l_pool.tile([P, NT], F32, name="l_sb")
                 l_sb[i] = t
                 nc.vector.tensor_tensor(out=t[:], in0=bank_l[i][:], in1=bl_all[:, gcols(i)], op=ALU.add)
 
@@ -457,23 +446,22 @@ def tile_llamaselfattentionblock_pb_l_kernel(tc, h_ffn, w1, b1, wg, bg, wl, bl, 
                 if i < n_steps2:
                     matmuls(i, 0, bank_g)
                     matmuls(i, 1, bank_l)
+                for job in copies.get(i, []):
+                    job_copy_scalar(job, 0, 1)
                 if i == n_steps2:
                     finish(i - 2)
                     gate_sigmoid(i - 1)
-                    add_bl_last(i - 1)
+                    add_bl(i - 1)
                     finish(i - 1)
                     break
-                if i >= 1:
-                    copy_l(i - 1)
-                for job, part in copies.get(i, []):
-                    job_copy_scalar(job, part, PACK)
                 if i >= 1:
                     add_bl(i - 1)
                 if i >= 2:
                     finish(i - 2)
-                add_bg(i)
-                sigmoid(i)
                 if i >= 1:
                     gate_lin(i - 1)
+                if i < n_steps2:
+                    add_bg(i)
+                    sigmoid(i)
                 for job in quants.get(i, []):
                     job_quant(job)

from contextlib import ExitStack

import concourse.mybir as mybir
from concourse.masks import make_identity

F32 = mybir.dt.float32
BF16 = mybir.dt.bfloat16
U32 = mybir.dt.uint32
U8 = mybir.dt.uint8
FP8X4 = mybir.dt.float8_e4m3fn_x4
ACT = mybir.ActivationFunctionType
ALU = mybir.AluOpType

P = 128
PACK = 4
KP = P * PACK
NT = 512

RAW_W_BUFS = 4
UST_BUFS = 2
LOAD_AHEAD = 1
S_PARTS_ROW0 = 2
S_PARTS = 1
BIAS_LOAD_STEP = 12


def v_units(i, n_blk):
    if i < n_blk:
        return 1
    return 1 if i % 3 else 0

FLOPS = 2 * 2560 * 1536 * 3072 + 2 * 2 * 2560 * 3072 * 3072


def tile_llamaselfattentionblock_pb_l_kernel(tc, h_ffn, w1, b1, wg, bg, wl, bl, beta, out):
    nc = tc.nc
    h2 = h_ffn.flatten_outer_dims()
    o2 = out.flatten_outer_dims()
    n_tok, e_dim = h2.shape
    f_dim = w1.shape[1]
    g_dim = wg.shape[1]
    n_blk = n_tok // NT
    n_mt = n_tok // P
    e_pass = e_dim // KP
    f_pass = f_dim // KP
    g_chunks = g_dim // NT

    n_steps1 = f_pass * n_blk
    n_steps2 = g_chunks * n_mt

    with ExitStack() as ctx:
        keep = ctx.enter_context(tc.tile_pool(name="keep", bufs=1))
        raw_w_pool = ctx.enter_context(tc.tile_pool(name="raw_w", bufs=RAW_W_BUFS))
        grp_wv_pool = ctx.enter_context(tc.tile_pool(name="grp_wv", bufs=2))
        grp_ws_pool = ctx.enter_context(tc.tile_pool(name="grp_ws", bufs=2))
        wca_pool = ctx.enter_context(tc.tile_pool(name="wca", bufs=2 * f_pass))
        wpa_pool = ctx.enter_context(tc.tile_pool(name="wpa", bufs=2))
        psum = ctx.enter_context(tc.psum_pool(name="psum", bufs=8))

        warm = keep.tile([P, 1], F32, name="warm")
        nc.vector.memset(warm[:], 0.0)
        nc.scalar.activation(out=warm[:], in_=warm[:], func=ACT.Sigmoid)
        ident = keep.tile([P, P], F32, name="ident")
        make_identity(nc, ident[:])
        b1_raw = keep.tile([P, f_pass, PACK], BF16, name="b1_raw")
        nc.scalar.dma_start(out=b1_raw[:], in_=b1.rearrange("(c p t) -> p c t", p=P, t=PACK))
        beta_raw = keep.tile([P, 1], BF16, name="beta_raw")
        nc.scalar.dma_start(out=beta_raw[:], in_=beta.partition_broadcast(P))
        b1_col = keep.tile([P, f_pass * PACK], F32, name="b1_col")
        beta_col = keep.tile([P, 1], F32, name="beta_col")
        bg_all = keep.tile([P, g_dim], BF16, name="bg_all")
        bl_all = keep.tile([P, g_dim], BF16, name="bl_all")

        u_codes = []
        for c in range(f_pass):
            uc = keep.tile([P, n_tok], U32, name="uc%d" % c, align_bytes=256)
            u_codes.append(uc)
        u_planes = []
        for c in range((f_pass + 3) // 4):
            up = keep.tile([P, n_tok], U8, name="up%d" % c, align_bytes=256)
            u_planes.append(up)

        ctx.enter_context(tc.manual_schedule())

        def quantize(grp, codes, plane):
            nc.vector.quantize_mx(out=codes.bitcast(FP8X4), scales=plane, in_=grp)

        def job_load(job):
            raw = raw_w_pool.tile([P, PACK, NT], BF16, name="raw_w")
            k0 = job["k_pass"] * KP
            nc.sync.dma_start(
                out=raw[:],
                in_=job["w"][k0 : k0 + KP, job["col0"] : job["col0"] + NT].rearrange("(p j) n -> p j n", j=PACK),
            )
            job["raw"] = raw

        def job_views(job, grp):
            if job["permute"]:
                dst = grp[:].rearrange("p (t m j) -> p t m j", t=PACK, j=PACK)
                src = job["raw"][:].rearrange("p j (m t) -> p t m j", t=PACK)
            else:
                dst = grp[:].rearrange("p (t m j) -> p t m j", t=PACK, j=PACK)
                src = job["raw"][:].rearrange("p j (t m) -> p t m j", t=PACK)
            return dst, src

        def job_copy_vector(job):
            grp = grp_wv_pool.tile([P, NT * PACK], BF16, name="grp_w", align_bytes=256)
            job["grp"] = grp
            dst, src = job_views(job, grp)
            nc.vector.tensor_copy(out=dst, in_=src)

        def job_copy_scalar(job, part, parts):
            if part == 0:
                grp = grp_ws_pool.tile([P, NT * PACK], BF16, name="grp_w", align_bytes=256)
                job["grp"] = grp
            dst, src = job_views(job, job["grp"])
            span = PACK // parts
            sel = slice(part * span, (part + 1) * span)
            nc.scalar.copy(out=dst[:, sel], in_=src[:, sel])

        def job_quant(job):
            codes, plane = job["target"]()
            quantize(job["grp"][:], codes[:], plane)

        chunks = {}

        def chunk_jobs(q, code_pool, plane_pool):
            chunks[q] = ({}, {})
            jobs = []
            for which, w in enumerate((wg, wl)):
                holder = {}

                def target(c, which=which, holder=holder):
                    if "planes" not in holder:
                        planes = plane_pool.tile([P, 2, NT], U8, name="wp", align_bytes=256)
                        holder["planes"] = planes
                    codes = code_pool.tile([P, NT], U32, name="wc", align_bytes=256)
                    plane = holder["planes"][4 * (c % 4) :, c // 4, :]
                    chunks[q][which][c] = (codes, plane)
                    return codes, plane

                for c in range(f_pass):
                    jobs.append(
                        {"w": w, "k_pass": c, "col0": q * NT, "permute": False, "target": lambda c=c, f=target: f(c)}
                    )
            return jobs

        with ExitStack() as s1:
            w1c_pool = s1.enter_context(tc.tile_pool(name="w1c", bufs=3 * e_pass))
            w1p_pool = s1.enter_context(tc.tile_pool(name="w1p", bufs=e_pass + 2))
            h_keep = s1.enter_context(tc.tile_pool(name="h_keep", bufs=1))
            raw_h_pool = s1.enter_context(tc.tile_pool(name="raw_h", bufs=6))
            grp_av_pool = s1.enter_context(tc.tile_pool(name="grp_av", bufs=2))
            grp_as_pool = s1.enter_context(tc.tile_pool(name="grp_as", bufs=3))
            ust_pool = s1.enter_context(tc.tile_pool(name="ust", bufs=UST_BUFS))

            h_codes = {}
            h_planes = {}
            for n in range(n_blk):
                hp = h_keep.tile([P, NT], U8, name="hp%d" % n, align_bytes=256)
                h_planes[n] = hp
                for g in range(e_pass):
                    hc = h_keep.tile([P, NT], U32, name="hc%d_%d" % (n, g), align_bytes=256)
                    h_codes[(n, g)] = hc

            w1_units = {}
            w1_planes = {}

            def w1_job(c, g):
                def target():
                    codes = w1c_pool.tile([P, NT], U32, name="w1c", align_bytes=256)
                    if c == 0:
                        planes = w1p_pool.tile([P, NT], U8, name="w1p", align_bytes=256)
                        plane = planes[:]
                    else:
                        if c not in w1_planes:
                            planes = w1p_pool.tile([P, NT], U8, name="w1p", align_bytes=256)
                            w1_planes[c] = planes
                        plane = w1_planes[c][4 * g :, :]
                    w1_units[(c, g)] = (codes, plane)
                    return codes, plane

                return {"w": w1, "k_pass": g, "col0": c * NT, "permute": True, "target": target, "chunk": c}

            h_raws = {}

            def h_load(hb):
                if hb >= 2 * n_blk:
                    return
                raws = []
                for a in range(2):
                    m = 2 * hb + a
                    hr = raw_h_pool.tile([P, e_dim], BF16, name="raw_h")
                    nc.sync.dma_start(out=hr[:], in_=h2[m * P : (m + 1) * P, :])
                    raws.append(hr)
                h_raws[hb] = raws

            def h_transpose(hb, share):
                todo = []
                n, b = hb // 2, hb % 2
                for g in range(e_pass):
                    xt = psum.tile([P, 2, 2, P], F32, name="ps")
                    for a in range(2):
                        words = h_raws[hb][a][:].bitcast(F32)
                        for u in range(2):
                            nc.tensor.transpose(xt[:, a, u, :], words[:, 256 * g + u : 256 * (g + 1) : 2], ident[:])
                    on_vector = share and g % 2 == 1
                    grp_pool = grp_av_pool if on_vector else grp_as_pool
                    grp = grp_pool.tile([P, NT * 2], BF16, name="grp_a", align_bytes=256)
                    dst = grp[:].bitcast(F32).rearrange("p (a r u) -> p a r u", a=2, u=2)
                    src = xt[:].rearrange("p a u r -> p a r u")
                    if on_vector:
                        nc.vector.tensor_copy(out=dst, in_=src)
                    else:
                        nc.scalar.copy(out=dst, in_=src)
                    cols = slice(256 * b, 256 * (b + 1))
                    todo.append((grp[:], h_codes[(n, g)][:, cols], h_planes[n][4 * g :, cols]))
                h_load(hb + 3)
                return todo

            usts = {}

            def pass1(i, t, g, ps):
                c, n = i // n_blk, i % n_blk
                cols = slice(P * t, P * (t + 1))
                codes, plane = w1_units[(c, g)]
                nc.tensor.matmul_mx(
                    out=ps[:],
                    lhsT=codes[:, cols].bitcast(FP8X4),
                    lhsT_scale=plane[:, cols],
                    rhs=h_codes[(n, g)][:].bitcast(FP8X4),
                    rhs_scale=h_planes[n][4 * g :, :],
                    start=(g == 0),
                    stop=(g == e_pass - 1),
                )

            def evacuate1(i, t, ps):
                col = PACK * (i // n_blk) + t
                nc.scalar.activation(
                    out=usts[i][:, t, :], in_=ps[:], func=ACT.Identity, bias=b1_col[:, col : col + 1]
                )

            def tile1(i):
                ust = ust_pool.tile([P, PACK, NT], BF16, name="ust")
                usts[i] = ust
                for t in range(PACK):
                    ps = psum.tile([P, NT], F32, name="ps")
                    for g in range(e_pass):
                        pass1(i, t, g, ps)
                    evacuate1(i, t, ps)

            u_grps = {}

            def u_interleave(i):
                grp = grp_av_pool.tile([P, NT * PACK], BF16, name="grp_a", align_bytes=256)
                u_grps[i] = grp
                nc.vector.tensor_copy(
                    out=grp[:].rearrange("p (n t) -> p n t", t=PACK), in_=usts[i][:].rearrange("p t n -> p n t")
                )

            def u_quant(i):
                c, n = i // n_blk, i % n_blk
                cols = slice(NT * n, NT * (n + 1))
                quantize(u_grps[i][:], u_codes[c][:, cols], u_planes[c // 4][4 * (c % 4) :, cols])

            w1_todo = [w1_job(c, g) for c in range(1, f_pass) for g in range(e_pass)]
            s2_todo = chunk_jobs(0, wca_pool, wpa_pool)

            taken = {"w1": 0, "s2": 0}

            def pop_job(i):
                a, b = taken["w1"], taken["s2"]
                if a < len(w1_todo) and i + 1 >= n_blk * (w1_todo[a]["chunk"] - 2):
                    taken["w1"] = a + 1
                    return w1_todo[a]
                if b < len(s2_todo):
                    taken["s2"] = b + 1
                    return s2_todo[b]
                return None

            loads = {}
            v_copy = {}
            s_copy = {}
            quants = {}
            s_job = None
            s_done = 0
            n_plan = n_steps1
            i = -1
            while i + 1 < n_plan:
                i += 1
                if i == n_plan - 1 and (taken["w1"] < len(w1_todo) or taken["s2"] < len(s2_todo) or s_job is not None):
                    n_plan += 1
                for k in range(S_PARTS_ROW0 if i < n_blk else S_PARTS):
                    if s_job is None:
                        s_job = pop_job(i)
                        s_done = 0
                        if s_job is not None:
                            loads[i - LOAD_AHEAD] = loads.get(i - LOAD_AHEAD, []) + [s_job]
                    if s_job is not None:
                        s_copy[i] = s_copy.get(i, []) + [(s_job, s_done)]
                        s_done += 1
                        if s_done == PACK:
                            quants[i + 1] = quants.get(i + 1, []) + [s_job]
                            s_job = None
                for k in range(v_units(i, n_blk)):
                    job = pop_job(i)
                    if job is not None:
                        loads[i - LOAD_AHEAD] = loads.get(i - LOAD_AHEAD, []) + [job]
                        v_copy[i] = v_copy.get(i, []) + [job]
                        quants[i + 1] = quants.get(i + 1, []) + [job]
            assert taken["w1"] == len(w1_todo) and taken["s2"] == len(s2_todo) and s_job is None

            first = [w1_job(0, g) for g in range(e_pass)]
            h_load(0)
            h_load(1)
            for job in first:
                job_load(job)
            h_load(2)
            nc.vector.tensor_copy(out=b1_col[:], in_=b1_raw[:].rearrange("p c t -> p (c t)"))
            nc.vector.tensor_copy(out=beta_col[:], in_=beta_raw[:])
            for hb in range(2):
                for args in h_transpose(hb, False):
                    quantize(*args)
            ust = ust_pool.tile([P, PACK, NT], BF16, name="ust")
            usts[0] = ust
            banks0 = []
            for t in range(PACK):
                ps = psum.tile([P, NT], F32, name="ps")
                banks0.append(ps)
            for g in range(e_pass):
                if g % 2 == 1:
                    job_copy_scalar(first[g], 0, 1)
                else:
                    job_copy_vector(first[g])
            for g in range(e_pass):
                job_quant(first[g])
                for t in range(PACK):
                    pass1(0, t, g, banks0[t])
            for t in range(PACK):
                evacuate1(0, t, banks0[t])
            for i in range(-LOAD_AHEAD, 0):
                for job in loads.get(i, []):
                    job_load(job)

            for i in range(n_plan + 1):
                for job in loads.get(i, []):
                    job_load(job)
                if i == min(BIAS_LOAD_STEP, n_steps1 - 1):
                    nc.sync.dma_start(out=bg_all[:], in_=bg.partition_broadcast(P))
                    nc.sync.dma_start(out=bl_all[:], in_=bl.partition_broadcast(P))
                if 0 < i < n_steps1:
                    tile1(i)
                if 0 < i <= n_steps1:
                    u_interleave(i - 1)
                for job in quants.get(i, []):
                    job_quant(job)
                if 0 < i <= n_steps1:
                    u_quant(i - 1)
                if i < n_blk:
                    for hb in range(3 * i + 2, min(3 * i + 5, 2 * n_blk)):
                        for args in h_transpose(hb, False):
                            quantize(*args)
                for job in v_copy.get(i, []):
                    job_copy_vector(job)
                for job, part in s_copy.get(i, []):
                    job_copy_scalar(job, part, PACK)

        with ExitStack() as s2:
            wcb_pool = s2.enter_context(tc.tile_pool(name="wcb", bufs=2 * f_pass))
            wpb_pool = s2.enter_context(tc.tile_pool(name="wpb", bufs=2))
            g_pool = s2.enter_context(tc.tile_pool(name="g_sb", bufs=2))
            l_pool = s2.enter_context(tc.tile_pool(name="l_sb", bufs=3))
            s_pool = s2.enter_context(tc.tile_pool(name="s_sb", bufs=4))

            loads = {}
            copies = {}
            quants = {}
            for q in range(1, g_chunks):
                if q % 2 == 0:
                    jobs = chunk_jobs(q, wca_pool, wpa_pool)
                else:
                    jobs = chunk_jobs(q, wcb_pool, wpb_pool)
                for j, job in enumerate(jobs):
                    i = (q - 1) * n_mt + (j * (n_mt - 2)) // len(jobs)
                    at = max(i - LOAD_AHEAD, 0)
                    loads[at] = loads.get(at, []) + [job]
                    copies[i] = copies.get(i, []) + [job]
                    quants[i + 1] = quants.get(i + 1, []) + [job]

            bank_g = {}
            bank_l = {}
            g_sb = {}
            l_sb = {}
            s_sb = {}

            def matmuls(i, which, banks):
                q, m = i // n_mt, i % n_mt
                tcols = slice(m * P, (m + 1) * P)
                ps = psum.tile([P, NT], F32, name="ps")
                banks[i] = ps
                for c in range(f_pass):
                    codes, plane = chunks[q][which][c]
                    nc.tensor.matmul_mx(
                        out=ps[:],
                        lhsT=u_codes[c][:, tcols].bitcast(FP8X4),
                        lhsT_scale=u_planes[c // 4][4 * (c % 4) :, tcols],
                        rhs=codes[:].bitcast(FP8X4),
                        rhs_scale=plane,
                        start=(c == 0),
                        stop=(c == f_pass - 1),
                    )

            def gcols(i):
                q = i // n_mt
                return slice(q * NT, (q + 1) * NT)

            def add_bg(i):
                t = g_pool.tile([P, NT], F32, name="g_sb")
                g_sb[i] = t
                nc.vector.tensor_tensor(out=t[:], in0=bank_g[i][:], in1=bg_all[:, gcols(i)], op=ALU.add)

            def sigmoid(i):
                t = s_pool.tile([P, NT], F32, name="s_sb")
                s_sb[i] = t
                nc.scalar.activation(out=t[:], in_=g_sb[i][:], func=ACT.Sigmoid, scale=beta_col[:, 0:1])

            def add_bl(i):
                t = l_pool.tile([P, NT], F32, name="l_sb")
                l_sb[i] = t
                nc.vector.tensor_tensor(out=t[:], in0=bank_l[i][:], in1=bl_all[:, gcols(i)], op=ALU.add)

            def gate_lin(i):
                nc.vector.tensor_tensor(out=l_sb[i][:], in0=g_sb[i][:], in1=l_sb[i][:], op=ALU.mult)

            def gate_sigmoid(i):
                nc.vector.tensor_tensor(out=s_sb[i][:], in0=g_sb[i][:], in1=s_sb[i][:], op=ALU.mult)

            def finish(i):
                m = i % n_mt
                nc.vector.tensor_tensor(out=s_sb[i][:], in0=l_sb[i][:], in1=s_sb[i][:], op=ALU.mult)
                nc.sync.dma_start(out=o2[m * P : (m + 1) * P, gcols(i)], in_=s_sb[i][:])

            for i in range(n_steps2 + 1):
                for job in loads.get(i, []):
                    job_load(job)
                if i < n_steps2:
                    matmuls(i, 0, bank_g)
                    matmuls(i, 1, bank_l)
                for job in copies.get(i, []):
                    job_copy_scalar(job, 0, 1)
                if i == n_steps2:
                    finish(i - 2)
                    gate_sigmoid(i - 1)
                    add_bl(i - 1)
                    finish(i - 1)
                    break
                if i >= 1:
                    add_bl(i - 1)
                if i >= 2:
                    finish(i - 2)
                if i >= 1:
                    gate_lin(i - 1)
                if i < n_steps2:
                    add_bg(i)
                    sigmoid(i)
                for job in quants.get(i, []):
                    job_quant(job)
